import numpy as np
import ml_dtypes


def mxq(x, axis, fmt="e4m3"):
    dtype, down = {"e4m3": (ml_dtypes.float8_e4m3fn, 7), "e5m2": (ml_dtypes.float8_e5m2, 14)}[fmt]
    v = np.moveaxis(np.asarray(x, np.float32).astype(ml_dtypes.bfloat16).astype(np.float64), axis, -1)
    blocks = v.reshape(v.shape[:-1] + (-1, 32))
    amax = np.abs(blocks).max(-1, keepdims=True)
    byte = np.maximum(np.where(amax > 0, np.frexp(amax)[1] - 1 + 127, 0) - down, 1)
    scale = np.exp2(byte - 127.0)
    codes = (blocks / scale).astype(np.float32).astype(dtype).astype(np.float64)
    return np.moveaxis((codes * scale).reshape(v.shape), -1, axis)


WIDE = False


def mx_kscale(k):
    if not WIDE:
        return np.ones(k)
    levels = np.array([10, -10, 5, -5, 0])
    a = np.random.permutation(np.resize(levels, k // 512 * 4)).reshape(k // 512, 4)
    idx = np.arange(k)
    return np.exp2(a[idx // 512, idx % 128 // 32])


BF16 = ml_dtypes.bfloat16


def bf(x):
    return np.asarray(x, np.float32).astype(BF16)


def f64(x):
    return np.asarray(x).astype(np.float64)


E2M1 = np.array([0.0, 0.5, 1.0, 1.5, 2.0, 3.0, 4.0, 6.0, -0.0, -0.5, -1.0, -1.5, -2.0, -3.0, -4.0, -6.0])


def pack_weight(w, fmt):
    k, n = w.shape
    w = f64(bf(w)).reshape(k // 32, 32, n)
    amax = np.abs(w).max(1)
    if fmt == "e4m3":
        byte = np.frexp(amax)[1] - 1 + 127 - 7
    else:
        mant, ex = np.frexp(amax / 6.0)
        byte = np.where(mant > 0.5, ex, ex - 1) + 127
    byte = np.clip(np.where(amax > 0, byte, 1), 1, 254)
    scaled = (w * np.exp2(127.0 - byte)[:, None, :]).reshape(k, n).astype(np.float32)
    by_word = np.ascontiguousarray(scaled.reshape(k // 512, 128, 4, n).transpose(0, 1, 3, 2))
    if fmt == "e4m3":
        words = by_word.astype(ml_dtypes.float8_e4m3fn).view(np.uint8)
    else:
        c = by_word.astype(ml_dtypes.float4_e2m1fn).view(np.uint8) & 0xF
        words = c[..., 0::2] | (c[..., 1::2] << 4)
    return np.ascontiguousarray(words), np.ascontiguousarray(byte.astype(np.uint8).reshape(k // 512, 16, n))


def unpack_weight(words, scales, fmt):
    g, p, n, _ = words.shape
    if fmt == "e4m3":
        vals = np.ascontiguousarray(words).view(ml_dtypes.float8_e4m3fn).astype(np.float64)
    else:
        nib = np.empty((g, p, n, 4), np.uint8)
        nib[..., 0::2] = words & 0xF
        nib[..., 1::2] = words >> 4
        vals = E2M1[nib]
    vals = vals * np.repeat(np.exp2(scales.astype(np.float64) - 127.0), 8, axis=1)[..., None]
    return vals.transpose(0, 1, 3, 2).reshape(g * 512, n)


B, Nb1, Nw1, Nb2x, Nb2y, Nw2x, Nw2y, R, C = 4096, 2, 16, 1, 1, 32, 16, 128, 2
J1 = Nb1 * Nb1
J3 = Nb2x * Nb2y
J2 = J3 * J1
K3 = J1 * R
L3 = C * Nw2x * Nw2y


def setup_inputs():
    t = mx_kscale(K3)
    tt = np.tile(t.reshape(J1, R), (J3, 1))
    h_switch = bf(np.random.standard_normal((B, J2, R)))
    k2 = bf(np.random.standard_normal((J2, R, R)) / np.sqrt(R) * tt[:, None, :])
    b2 = bf(np.random.standard_normal((1, J2, R)) * 0.3 * tt[None])
    k3 = np.random.standard_normal((J3, K3, L3)) / np.sqrt(K3) / t[None, :, None]
    k3_words, k3_scales = pack_weight(k3.reshape(-1, L3), "e4m3")
    b3 = bf(np.random.standard_normal((1, J3, L3)) * 0.3)
    return {"h_switch": h_switch,
            "k2": k2,
            "b2": b2,
            "k3_words": k3_words,
            "k3_scales": k3_scales,
            "b3": b3}


def reference(h_switch, k2, b2, k3_words, k3_scales, b3):
    g = (f64(h_switch).transpose(1, 0, 2) @ f64(k2)).transpose(1, 0, 2) + f64(b2)
    g = g.reshape(B, J3, K3)
    gq = mxq(g, 2, "e4m3").transpose(1, 0, 2)
    k3q = unpack_weight(k3_words, k3_scales, "e4m3").reshape(J3, K3, L3)
    y = (gq @ k3q).transpose(1, 0, 2) + f64(b3)
    y = y.reshape(B, Nb2x, Nb2y, Nw2x, Nw2y, C).transpose(0, 1, 3, 2, 4, 5)
    return y.reshape(B, Nb2x * Nw2x, Nb2y * Nw2y, C)

@@ -1,0 +1,204 @@
+from contextlib import ExitStack
+
+import concourse.mybir as mybir
+from concourse.masks import make_identity
+
+F32 = mybir.dt.float32
+BF16 = mybir.dt.bfloat16
+I32 = mybir.dt.int32
+U32 = mybir.dt.uint32
+U8 = mybir.dt.uint8
+FP8X4 = mybir.dt.float8_e4m3fn_x4
+ADD = mybir.AluOpType.add
+
+P = 128
+BATCH = 4096
+GROUPS = 4
+R = 128
+K3 = GROUPS * R
+L3 = 1024
+BANK = 512
+HALVES = L3 // BANK
+PAIRS = 2
+
+CHUNK_TILES = 8
+CHUNKS = BATCH // (P * CHUNK_TILES)
+ROUND_TILES = 2
+CHUNK_ROUNDS = CHUNK_TILES // ROUND_TILES
+ROUNDS = CHUNKS * CHUNK_ROUNDS
+
+FLOPS = 2 * BATCH * (GROUPS * R * R + K3 * L3)
+
+
+def tile_switchnet_fstar_pb_t_e_kernel(tc, h_switch, k2, b2, k3_words, k3_scales, b3, out):
+    nc = tc.nc
+    h_chunks = h_switch.rearrange("(n p c) j i -> n p c (j i)", p=P, c=CHUNK_TILES)
+    out_chunks = out.rearrange("(n p c) x y z -> n p c (x y z)", p=P, c=CHUNK_TILES)
+
+    with ExitStack() as ctx:
+        keep = ctx.enter_context(tc.tile_pool(name="keep", bufs=1))
+        ht_pool = ctx.enter_context(tc.tile_pool(name="ht", bufs=3))
+        g_pool = ctx.enter_context(tc.tile_pool(name="g", bufs=3))
+        grouped_pool = ctx.enter_context(tc.tile_pool(name="grouped", bufs=2))
+        mx_pool = ctx.enter_context(tc.tile_pool(name="mx", bufs=3))
+        y_pool = ctx.enter_context(tc.tile_pool(name="y", bufs=4))
+        psum_ht = ctx.enter_context(tc.psum_pool(name="psum_ht", bufs=1))
+        psum_g = ctx.enter_context(tc.psum_pool(name="psum_g", bufs=ROUND_TILES))
+        psum_gt = ctx.enter_context(tc.psum_pool(name="psum_gt", bufs=1))
+        psum_y = ctx.enter_context(tc.psum_pool(name="psum_y", bufs=ROUND_TILES * HALVES))
+        ctx.enter_context(tc.manual_schedule())
+
+        h_sb = keep.tile([P, CHUNKS, CHUNK_TILES, K3], BF16)
+        k2_sb = keep.tile([P, GROUPS, R], BF16)
+        k3_codes = keep.tile([P, L3], U32, align_bytes=64)
+        k3_plane = keep.tile([P, L3], U8, align_bytes=64)
+        b2_rows = keep.tile([P, K3], BF16)
+        b3_rows = keep.tile([P, L3], BF16)
+        b2_sorted = keep.tile([P, K3], F32)
+        b3_f32 = keep.tile([P, L3], F32)
+        ident_bf16 = keep.tile([P, P], BF16)
+        ident_f32 = keep.tile([P, P], F32)
+
+        def load_h(n, first_tile, tiles):
+            cols = slice(first_tile, first_tile + tiles)
+            nc.sync.dma_start(out=h_sb[:, n, cols, :], in_=h_chunks[n][:, cols, :])
+
+        nc.vector.memset(k3_plane[:].bitcast(I32), 0)
+        make_identity(nc, ident_bf16[:])
+        make_identity(nc, ident_f32[:])
+
+        nc.scalar.dma_start(out=b2_rows[:], in_=b2.rearrange("o j r -> (o j r)").partition_broadcast(P))
+        nc.scalar.dma_start(out=b3_rows[:], in_=b3.rearrange("o j l -> (o j l)").partition_broadcast(P))
+
+        load_h(0, 0, ROUND_TILES)
+        nc.sync.dma_start(out=k2_sb[:], in_=k2.rearrange("j i r -> i j r"))
+        load_h(0, ROUND_TILES, ROUND_TILES)
+        for quadrant in range(4):
+            nc.sync.dma_start(
+                out=k3_plane[32 * quadrant : 32 * quadrant + 4, :].bitcast(I32),
+                in_=k3_scales[0, 4 * quadrant : 4 * quadrant + 4, :].bitcast(I32),
+            )
+        nc.sync.dma_start(
+            out=k3_codes[:].bitcast(I32),
+            in_=k3_words[0].rearrange("p n t -> p (n t)").bitcast(I32),
+        )
+        for r in range(2, CHUNK_ROUNDS):
+            load_h(0, r * ROUND_TILES, ROUND_TILES)
+        for n in range(1, CHUNKS):
+            load_h(n, 0, CHUNK_TILES)
+
+        nc.vector.tensor_copy(
+            out=b2_sorted[:].rearrange("b (u p e) -> b u p e", u=PAIRS, e=2),
+            in_=b2_rows[:].rearrange("b (p u e) -> b u p e", u=PAIRS, e=2),
+        )
+        nc.vector.tensor_copy(out=b3_f32[:], in_=b3_rows[:])
+
+        ht_of = {}
+        g_of = {}
+        grouped_of = {}
+        codes_of = {}
+        plane_of = {}
+
+        def transpose_h(r):
+            n, q = divmod(r, CHUNK_ROUNDS)
+            ht_ps = psum_ht.tile([P, ROUND_TILES, GROUPS, P], BF16)
+            for c in range(ROUND_TILES):
+                for j in range(GROUPS):
+                    nc.tensor.transpose(
+                        ht_ps[:, c, j, :],
+                        h_sb[:, n, q * ROUND_TILES + c, j * R : (j + 1) * R],
+                        ident_bf16[:],
+                    )
+            ht = ht_pool.tile([P, ROUND_TILES, GROUPS, P], BF16)
+            nc.scalar.copy(out=ht[:], in_=ht_ps[:])
+            ht_of[r] = ht
+
+        def first_matmul(r):
+            ht = ht_of[r]
+            g = g_pool.tile([P, ROUND_TILES, K3], BF16)
+            for c in range(ROUND_TILES):
+                g_ps = psum_g.tile([P, K3], F32)
+                for j in range(GROUPS):
+                    nc.tensor.matmul(
+                        g_ps[:, j * R : (j + 1) * R],
+                        lhsT=ht[:, c, j, :],
+                        rhs=k2_sb[:, j, :],
+                        start=True,
+                        stop=True,
+                    )
+                nc.vector.tensor_tensor(
+                    out=g[:, c, :].rearrange("b (u p e) -> b u p e", u=PAIRS, e=2),
+                    in0=g_ps[:].rearrange("b (p u e) -> b u p e", u=PAIRS, e=2),
+                    in1=b2_sorted[:].rearrange("b (u p e) -> b u p e", u=PAIRS, e=2),
+                    op=ADD,
+                )
+            g_of[r] = g
+
+        def transpose_g(r):
+            g = g_of[r]
+            gt_ps = psum_gt.tile([P, ROUND_TILES, PAIRS, P], F32)
+            for c in range(ROUND_TILES):
+                g_words = g[:, c, :].bitcast(F32)
+                for u in range(PAIRS):
+                    nc.tensor.transpose(gt_ps[:, c, u, :], g_words[:, u * P : (u + 1) * P], ident_f32[:])
+            grouped = grouped_pool.tile([P, ROUND_TILES * P * 4], BF16, align_bytes=64)
+            nc.scalar.copy(
+                out=grouped[:].bitcast(F32).rearrange("p (c b u) -> p c b u", c=ROUND_TILES, u=PAIRS),
+                in_=gt_ps[:].rearrange("p c u b -> p c b u"),
+            )
+            grouped_of[r] = grouped
+
+        def quantise(r):
+            grouped = grouped_of[r]
+            g_codes = mx_pool.tile([P, ROUND_TILES * P], U32, align_bytes=64)
+            g_plane = mx_pool.tile([P, ROUND_TILES * P], U8, align_bytes=64)
+            nc.vector.quantize_mx(out=g_codes[:].bitcast(FP8X4), scales=g_plane[:], in_=grouped[:])
+            codes_of[r] = g_codes
+            plane_of[r] = g_plane
+
+        def second_matmul(r):
+            n, q = divmod(r, CHUNK_ROUNDS)
+            g_codes = codes_of[r]
+            g_plane = plane_of[r]
+            y = y_pool.tile([P, ROUND_TILES, L3], F32)
+            for c in range(ROUND_TILES):
+                samples = slice(c * P, (c + 1) * P)
+                for half in range(HALVES):
+                    cols = slice(half * BANK, (half + 1) * BANK)
+                    y_ps = psum_y.tile([P, BANK], F32)
+                    nc.tensor.matmul_mx(
+                        out=y_ps[:],
+                        lhsT=g_codes[:, samples].bitcast(FP8X4),
+                        lhsT_scale=g_plane[:, samples],
+                        rhs=k3_codes[:, cols].bitcast(FP8X4),
+                        rhs_scale=k3_plane[:, cols],
+                        start=True,
+                        stop=True,
+                    )
+                    if half == 0:
+                        nc.vector.tensor_tensor(out=y[:, c, cols], in0=y_ps[:], in1=b3_f32[:, cols], op=ADD)
+                    else:
+                        nc.scalar.copy(out=y[:, c, cols], in_=y_ps[:])
+            nc.gpsimd.tensor_tensor(
+                out=y[:, :, BANK:],
+                in0=y[:, :, BANK:],
+                in1=b3_f32[:, BANK:].unsqueeze(1).to_broadcast([P, ROUND_TILES, BANK]),
+                op=ADD,
+            )
+            tiles = slice(q * ROUND_TILES, (q + 1) * ROUND_TILES)
+            nc.sync.dma_start(out=out_chunks[n][:, tiles, :], in_=y[:])
+
+        def due(r):
+            return 0 <= r < ROUNDS
+
+        for step in range(ROUNDS + 3):
+            if due(step):
+                transpose_h(step)
+            if due(step - 2):
+                transpose_g(step - 2)
+            if due(step - 1):
+                first_matmul(step - 1)
+            if due(step - 2):
+                quantise(step - 2)
+            if due(step - 3):
+                second_matmul(step - 3)

@@ -175,16 +175,7 @@ def tile_switchnet_fstar_pb_t_e_kernel(tc, h_switch, k2, b2, k3_words, k3_scales
                         start=True,
                         stop=True,
                     )
-                    if half == 0:
-                        nc.vector.tensor_tensor(out=y[:, c, cols], in0=y_ps[:], in1=b3_f32[:, cols], op=ADD)
-                    else:
-                        nc.scalar.copy(out=y[:, c, cols], in_=y_ps[:])
-            nc.gpsimd.tensor_tensor(
-                out=y[:, :, BANK:],
-                in0=y[:, :, BANK:],
-                in1=b3_f32[:, BANK:].unsqueeze(1).to_broadcast([P, ROUND_TILES, BANK]),
-                op=ADD,
-            )
+                    nc.vector.tensor_tensor(out=y[:, c, cols], in0=y_ps[:], in1=b3_f32[:, cols], op=ADD)
             tiles = slice(q * ROUND_TILES, (q + 1) * ROUND_TILES)
             nc.sync.dma_start(out=out_chunks[n][:, tiles, :], in_=y[:])
 

@@ -26,6 +26,7 @@ CHUNKS = BATCH // (P * CHUNK_TILES)
 ROUND_TILES = 2
 CHUNK_ROUNDS = CHUNK_TILES // ROUND_TILES
 ROUNDS = CHUNKS * CHUNK_ROUNDS
+TENSOR_BIAS_TILE = 1
 
 FLOPS = 2 * BATCH * (GROUPS * R * R + K3 * L3)
 
@@ -58,16 +59,21 @@ def tile_switchnet_fstar_pb_t_e_kernel(tc, h_switch, k2, b2, k3_words, k3_scales
         b3_f32 = keep.tile([P, L3], F32)
         ident_bf16 = keep.tile([P, P], BF16)
         ident_f32 = keep.tile([P, P], F32)
+        ones = keep.tile([P, P], BF16)
+        b2_row0 = keep.tile([P, K3], BF16)
 
         def load_h(n, first_tile, tiles):
             cols = slice(first_tile, first_tile + tiles)
             nc.sync.dma_start(out=h_sb[:, n, cols, :], in_=h_chunks[n][:, cols, :])
 
         nc.vector.memset(k3_plane[:].bitcast(I32), 0)
+        nc.vector.memset(b2_row0[:], 0.0)
+        nc.vector.memset(ones[:], 1.0)
         make_identity(nc, ident_bf16[:])
         make_identity(nc, ident_f32[:])
 
         nc.scalar.dma_start(out=b2_rows[:], in_=b2.rearrange("o j r -> (o j r)").partition_broadcast(P))
+        nc.scalar.dma_start(out=b2_row0[0:1, :], in_=b2.rearrange("o j r -> o (j r)"))
         nc.scalar.dma_start(out=b3_rows[:], in_=b3.rearrange("o j l -> (o j l)").partition_broadcast(P))
 
         load_h(0, 0, ROUND_TILES)
@@ -118,20 +124,28 @@ def tile_switchnet_fstar_pb_t_e_kernel(tc, h_switch, k2, b2, k3_words, k3_scales
             g = g_pool.tile([P, ROUND_TILES, K3], BF16)
             for c in range(ROUND_TILES):
                 g_ps = psum_g.tile([P, K3], F32)
+                tensor_adds_b2 = c == TENSOR_BIAS_TILE
+                if tensor_adds_b2:
+                    nc.tensor.matmul(g_ps[:], lhsT=ones[:], rhs=b2_row0[:], start=True, stop=False)
                 for j in range(GROUPS):
                     nc.tensor.matmul(
                         g_ps[:, j * R : (j + 1) * R],
                         lhsT=ht[:, c, j, :],
                         rhs=k2_sb[:, j, :],
-                        start=True,
-                        stop=True,
+                        start=not tensor_adds_b2,
+                        stop=not tensor_adds_b2 or j == GROUPS - 1,
                     )
-                nc.vector.tensor_tensor(
-                    out=g[:, c, :].rearrange("b (u p e) -> b u p e", u=PAIRS, e=2),
-                    in0=g_ps[:].rearrange("b (p u e) -> b u p e", u=PAIRS, e=2),
-                    in1=b2_sorted[:].rearrange("b (u p e) -> b u p e", u=PAIRS, e=2),
-                    op=ADD,
-                )
+                g_sorted = g[:, c, :].rearrange("b (u p e) -> b u p e", u=PAIRS, e=2)
+                g_ps_sorted = g_ps[:].rearrange("b (p u e) -> b u p e", u=PAIRS, e=2)
+                if tensor_adds_b2:
+                    nc.scalar.copy(out=g_sorted, in_=g_ps_sorted)
+                else:
+                    nc.vector.tensor_tensor(
+                        out=g_sorted,
+                        in0=g_ps_sorted,
+                        in1=b2_sorted[:].rearrange("b (u p e) -> b u p e", u=PAIRS, e=2),
+                        op=ADD,
+                    )
             g_of[r] = g
 
         def transpose_g(r):
@@ -175,7 +189,11 @@ def tile_switchnet_fstar_pb_t_e_kernel(tc, h_switch, k2, b2, k3_words, k3_scales
                         start=True,
                         stop=True,
                     )
-                    nc.vector.tensor_tensor(out=y[:, c, cols], in0=y_ps[:], in1=b3_f32[:, cols], op=ADD)
+                    if c == 0 and half == 0:
+                        nc.scalar.copy(out=y[:, c, cols], in_=y_ps[:])
+                        nc.gpsimd.tensor_tensor(out=y[:, c, cols], in0=y[:, c, cols], in1=b3_f32[:, cols], op=ADD)
+                    else:
+                        nc.vector.tensor_tensor(out=y[:, c, cols], in0=y_ps[:], in1=b3_f32[:, cols], op=ADD)
             tiles = slice(q * ROUND_TILES, (q + 1) * ROUND_TILES)
             nc.sync.dma_start(out=out_chunks[n][:, tiles, :], in_=y[:])
 

@@ -39,7 +39,7 @@ def tile_switchnet_fstar_pb_t_e_kernel(tc, h_switch, k2, b2, k3_words, k3_scales
     with ExitStack() as ctx:
         keep = ctx.enter_context(tc.tile_pool(name="keep", bufs=1))
         ht_pool = ctx.enter_context(tc.tile_pool(name="ht", bufs=3))
-        g_pool = ctx.enter_context(tc.tile_pool(name="g", bufs=3))
+        g_pool = ctx.enter_context(tc.tile_pool(name="g", bufs=4))
         grouped_pool = ctx.enter_context(tc.tile_pool(name="grouped", bufs=2))
         mx_pool = ctx.enter_context(tc.tile_pool(name="mx", bufs=3))
         y_pool = ctx.enter_context(tc.tile_pool(name="y", bufs=4))
@@ -119,10 +119,13 @@ def tile_switchnet_fstar_pb_t_e_kernel(tc, h_switch, k2, b2, k3_words, k3_scales
             nc.scalar.copy(out=ht[:], in_=ht_ps[:])
             ht_of[r] = ht
 
-        def first_matmul(r):
+        def first_matmul(r, tiles_of_round):
             ht = ht_of[r]
-            g = g_pool.tile([P, ROUND_TILES, K3], BF16)
-            for c in range(ROUND_TILES):
+            if r not in g_of:
+                g_new = g_pool.tile([P, ROUND_TILES, K3], BF16)
+                g_of[r] = g_new
+            g = g_of[r]
+            for c in tiles_of_round:
                 g_ps = psum_g.tile([P, K3], F32)
                 tensor_adds_b2 = c == TENSOR_BIAS_TILE
                 if tensor_adds_b2:
@@ -146,7 +149,6 @@ def tile_switchnet_fstar_pb_t_e_kernel(tc, h_switch, k2, b2, k3_words, k3_scales
                         in1=b2_sorted[:].rearrange("b (u p e) -> b u p e", u=PAIRS, e=2),
                         op=ADD,
                     )
-            g_of[r] = g
 
         def transpose_g(r):
             g = g_of[r]
@@ -200,14 +202,16 @@ def tile_switchnet_fstar_pb_t_e_kernel(tc, h_switch, k2, b2, k3_words, k3_scales
         def due(r):
             return 0 <= r < ROUNDS
 
-        for step in range(ROUNDS + 3):
+        for step in range(ROUNDS + 4):
             if due(step):
                 transpose_h(step)
-            if due(step - 2):
-                transpose_g(step - 2)
-            if due(step - 1):
-                first_matmul(step - 1)
-            if due(step - 2):
-                quantise(step - 2)
             if due(step - 3):
-                second_matmul(step - 3)
+                transpose_g(step - 3)
+            if due(step - 1):
+                first_matmul(step - 1, (0,))
+            if due(step - 3):
+                quantise(step - 3)
+            if due(step - 4):
+                second_matmul(step - 4)
+            if due(step - 1):
+                first_matmul(step - 1, (1,))

@@ -100,69 +100,101 @@ def tile_switchnet_fstar_pb_t_e_kernel(tc, h_switch, k2, b2, k3_words, k3_scales
         nc.vector.tensor_copy(out=b3_f32[:], in_=b3_rows[:])
 
         ht_of = {}
+        ht_ps_of = {}
+        g_ps_of = {}
+        gt_ps_of = {}
         g_of = {}
         grouped_of = {}
         codes_of = {}
         plane_of = {}
 
-        def transpose_h(r):
+        def transposes_of_h(r):
             n, q = divmod(r, CHUNK_ROUNDS)
             ht_ps = psum_ht.tile([P, ROUND_TILES, GROUPS, P], BF16)
-            for c in range(ROUND_TILES):
-                for j in range(GROUPS):
-                    nc.tensor.transpose(
-                        ht_ps[:, c, j, :],
-                        h_sb[:, n, q * ROUND_TILES + c, j * R : (j + 1) * R],
-                        ident_bf16[:],
-                    )
+            ht_ps_of[r] = ht_ps
+
+            def one(c, j):
+                nc.tensor.transpose(
+                    ht_ps[:, c, j, :],
+                    h_sb[:, n, q * ROUND_TILES + c, j * R : (j + 1) * R],
+                    ident_bf16[:],
+                )
+
+            return [(one, c, j) for c in range(ROUND_TILES) for j in range(GROUPS)]
+
+        def copy_ht(r):
             ht = ht_pool.tile([P, ROUND_TILES, GROUPS, P], BF16)
-            nc.scalar.copy(out=ht[:], in_=ht_ps[:])
+            nc.scalar.copy(out=ht[:], in_=ht_ps_of[r][:])
             ht_of[r] = ht
 
-        def first_matmul(r, tiles_of_round):
+        def products_of(r, c):
             ht = ht_of[r]
+            g_ps = psum_g.tile([P, K3], F32)
+            g_ps_of[r, c] = g_ps
+            tensor_adds_b2 = c == TENSOR_BIAS_TILE
+
+            def bias():
+                nc.tensor.matmul(g_ps[:], lhsT=ones[:], rhs=b2_row0[:], start=True, stop=False)
+
+            def one(j):
+                nc.tensor.matmul(
+                    g_ps[:, j * R : (j + 1) * R],
+                    lhsT=ht[:, c, j, :],
+                    rhs=k2_sb[:, j, :],
+                    start=not tensor_adds_b2,
+                    stop=not tensor_adds_b2 or j == GROUPS - 1,
+                )
+
+            return ([(bias,)] if tensor_adds_b2 else []), [(one, j) for j in range(GROUPS)]
+
+        def take_g(r, c):
             if r not in g_of:
                 g_new = g_pool.tile([P, ROUND_TILES, K3], BF16)
                 g_of[r] = g_new
             g = g_of[r]
-            for c in tiles_of_round:
-                g_ps = psum_g.tile([P, K3], F32)
-                tensor_adds_b2 = c == TENSOR_BIAS_TILE
-                if tensor_adds_b2:
-                    nc.tensor.matmul(g_ps[:], lhsT=ones[:], rhs=b2_row0[:], start=True, stop=False)
-                for j in range(GROUPS):
-                    nc.tensor.matmul(
-                        g_ps[:, j * R : (j + 1) * R],
-                        lhsT=ht[:, c, j, :],
-                        rhs=k2_sb[:, j, :],
-                        start=not tensor_adds_b2,
-                        stop=not tensor_adds_b2 or j == GROUPS - 1,
-                    )
-                g_sorted = g[:, c, :].rearrange("b (u p e) -> b u p e", u=PAIRS, e=2)
-                g_ps_sorted = g_ps[:].rearrange("b (p u e) -> b u p e", u=PAIRS, e=2)
-                if tensor_adds_b2:
-                    nc.scalar.copy(out=g_sorted, in_=g_ps_sorted)
-                else:
-                    nc.vector.tensor_tensor(
-                        out=g_sorted,
-                        in0=g_ps_sorted,
-                        in1=b2_sorted[:].rearrange("b (u p e) -> b u p e", u=PAIRS, e=2),
-                        op=ADD,
-                    )
+            g_ps = g_ps_of[r, c]
+            g_sorted = g[:, c, :].rearrange("b (u p e) -> b u p e", u=PAIRS, e=2)
+            g_ps_sorted = g_ps[:].rearrange("b (p u e) -> b u p e", u=PAIRS, e=2)
+            if c == TENSOR_BIAS_TILE:
+                nc.scalar.copy(out=g_sorted, in_=g_ps_sorted)
+            else:
+                nc.vector.tensor_tensor(
+                    out=g_sorted,
+                    in0=g_ps_sorted,
+                    in1=b2_sorted[:].rearrange("b (u p e) -> b u p e", u=PAIRS, e=2),
+                    op=ADD,
+                )
 
-        def transpose_g(r):
+        def transposes_of_g(r):
             g = g_of[r]
             gt_ps = psum_gt.tile([P, ROUND_TILES, PAIRS, P], F32)
-            for c in range(ROUND_TILES):
+            gt_ps_of[r] = gt_ps
+
+            def one(c, u):
                 g_words = g[:, c, :].bitcast(F32)
-                for u in range(PAIRS):
-                    nc.tensor.transpose(gt_ps[:, c, u, :], g_words[:, u * P : (u + 1) * P], ident_f32[:])
+                nc.tensor.transpose(gt_ps[:, c, u, :], g_words[:, u * P : (u + 1) * P], ident_f32[:])
+
+            return [(one, c, u) for c in range(ROUND_TILES) for u in range(PAIRS)]
+
+        def copy_gt(r):
             grouped = grouped_pool.tile([P, ROUND_TILES * P * 4], BF16, align_bytes=64)
             nc.scalar.copy(
                 out=grouped[:].bitcast(F32).rearrange("p (c b u) -> p c b u", c=ROUND_TILES, u=PAIRS),
-                in_=gt_ps[:].rearrange("p c u b -> p c b u"),
+                in_=gt_ps_of[r][:].rearrange("p c u b -> p c b u"),
             )
             grouped_of[r] = grouped
+
+        def issue(calls):
+            for call in calls:
+                call[0](*call[1:])
+
+        def woven(transposes, matmuls):
+            share = len(transposes) // len(matmuls)
+            out_list = []
+            for k in range(len(matmuls)):
+                out_list.extend(transposes[k * share : (k + 1) * share])
+                out_list.append(matmuls[k])
+            return out_list
 
         def quantise(r):
             grouped = grouped_of[r]
@@ -203,15 +235,27 @@ def tile_switchnet_fstar_pb_t_e_kernel(tc, h_switch, k2, b2, k3_words, k3_scales
             return 0 <= r < ROUNDS
 
         for step in range(ROUNDS + 4):
-            if due(step):
-                transpose_h(step)
-            if due(step - 3):
-                transpose_g(step - 3)
+            t_h = transposes_of_h(step) if due(step) else []
             if due(step - 1):
-                first_matmul(step - 1, (0,))
+                opening, products = products_of(step - 1, 0)
+                issue(opening + (woven(t_h, products) if t_h else products))
+            else:
+                issue(t_h)
+            if due(step):
+                copy_ht(step)
+            if due(step - 1):
+                take_g(step - 1, 0)
             if due(step - 3):
                 quantise(step - 3)
             if due(step - 4):
                 second_matmul(step - 4)
+            t_g = transposes_of_g(step - 2) if due(step - 2) else []
             if due(step - 1):
-                first_matmul(step - 1, (1,))
+                opening, products = products_of(step - 1, 1)
+                issue(opening + (woven(t_g, products) if t_g else products))
+            else:
+                issue(t_g)
+            if due(step - 2):
+                copy_gt(step - 2)
+            if due(step - 1):
+                take_g(step - 1, 1)

@@ -27,6 +27,7 @@ ROUND_TILES = 2
 CHUNK_ROUNDS = CHUNK_TILES // ROUND_TILES
 ROUNDS = CHUNKS * CHUNK_ROUNDS
 TENSOR_BIAS_TILE = 1
+SPREADS = 3
 
 FLOPS = 2 * BATCH * (GROUPS * R * R + K3 * L3)
 
@@ -53,14 +54,13 @@ def tile_switchnet_fstar_pb_t_e_kernel(tc, h_switch, k2, b2, k3_words, k3_scales
         k2_sb = keep.tile([P, GROUPS, R], BF16)
         k3_codes = keep.tile([P, L3], U32, align_bytes=64)
         k3_plane = keep.tile([P, L3], U8, align_bytes=64)
-        b2_rows = keep.tile([P, K3], BF16)
-        b3_rows = keep.tile([P, L3], BF16)
         b2_sorted = keep.tile([P, K3], F32)
         b3_f32 = keep.tile([P, L3], F32)
         ident_bf16 = keep.tile([P, P], BF16)
         ident_f32 = keep.tile([P, P], F32)
         ones = keep.tile([P, P], BF16)
         b2_row0 = keep.tile([P, K3], BF16)
+        b3_row0 = keep.tile([P, L3], BF16)
 
         def load_h(n, first_tile, tiles):
             cols = slice(first_tile, first_tile + tiles)
@@ -68,13 +68,13 @@ def tile_switchnet_fstar_pb_t_e_kernel(tc, h_switch, k2, b2, k3_words, k3_scales
 
         nc.vector.memset(k3_plane[:].bitcast(I32), 0)
         nc.vector.memset(b2_row0[:], 0.0)
+        nc.vector.memset(b3_row0[:], 0.0)
         nc.vector.memset(ones[:], 1.0)
         make_identity(nc, ident_bf16[:])
         make_identity(nc, ident_f32[:])
 
-        nc.scalar.dma_start(out=b2_rows[:], in_=b2.rearrange("o j r -> (o j r)").partition_broadcast(P))
         nc.scalar.dma_start(out=b2_row0[0:1, :], in_=b2.rearrange("o j r -> o (j r)"))
-        nc.scalar.dma_start(out=b3_rows[:], in_=b3.rearrange("o j l -> (o j l)").partition_broadcast(P))
+        nc.scalar.dma_start(out=b3_row0[0:1, :], in_=b3.rearrange("o j l -> o (j l)"))
 
         load_h(0, 0, ROUND_TILES)
         nc.sync.dma_start(out=k2_sb[:], in_=k2.rearrange("j i r -> i j r"))
@@ -93,11 +93,20 @@ def tile_switchnet_fstar_pb_t_e_kernel(tc, h_switch, k2, b2, k3_words, k3_scales
         for n in range(1, CHUNKS):
             load_h(n, 0, CHUNK_TILES)
 
-        nc.vector.tensor_copy(
-            out=b2_sorted[:].rearrange("b (u p e) -> b u p e", u=PAIRS, e=2),
-            in_=b2_rows[:].rearrange("b (p u e) -> b u p e", u=PAIRS, e=2),
-        )
-        nc.vector.tensor_copy(out=b3_f32[:], in_=b3_rows[:])
+        def spread_b2():
+            y_ps = psum_y.tile([P, BANK], F32)
+            nc.tensor.matmul(y_ps[:], lhsT=ones[:], rhs=b2_row0[:], start=True, stop=True)
+            nc.vector.tensor_copy(
+                out=b2_sorted[:].rearrange("b (u p e) -> b u p e", u=PAIRS, e=2),
+                in_=y_ps[:].rearrange("b (p u e) -> b u p e", u=PAIRS, e=2),
+            )
+
+        def spread_b3():
+            for half in range(HALVES):
+                cols = slice(half * BANK, (half + 1) * BANK)
+                y_ps = psum_y.tile([P, BANK], F32)
+                nc.tensor.matmul(y_ps[:], lhsT=ones[:], rhs=b3_row0[:, cols], start=True, stop=True)
+                nc.vector.tensor_copy(out=b3_f32[:, cols], in_=y_ps[:])
 
         ht_of = {}
         ht_ps_of = {}
@@ -131,7 +140,7 @@ def tile_switchnet_fstar_pb_t_e_kernel(tc, h_switch, k2, b2, k3_words, k3_scales
             ht = ht_of[r]
             g_ps = psum_g.tile([P, K3], F32)
             g_ps_of[r, c] = g_ps
-            tensor_adds_b2 = c == TENSOR_BIAS_TILE
+            tensor_adds_b2 = c == TENSOR_BIAS_TILE and r >= SPREADS
 
             def bias():
                 nc.tensor.matmul(g_ps[:], lhsT=ones[:], rhs=b2_row0[:], start=True, stop=False)
@@ -155,7 +164,7 @@ def tile_switchnet_fstar_pb_t_e_kernel(tc, h_switch, k2, b2, k3_words, k3_scales
             g_ps = g_ps_of[r, c]
             g_sorted = g[:, c, :].rearrange("b (u p e) -> b u p e", u=PAIRS, e=2)
             g_ps_sorted = g_ps[:].rearrange("b (p u e) -> b u p e", u=PAIRS, e=2)
-            if c == TENSOR_BIAS_TILE:
+            if c == TENSOR_BIAS_TILE and r >= SPREADS:
                 nc.scalar.copy(out=g_sorted, in_=g_ps_sorted)
             else:
                 nc.vector.tensor_tensor(
@@ -241,6 +250,10 @@ def tile_switchnet_fstar_pb_t_e_kernel(tc, h_switch, k2, b2, k3_words, k3_scales
                 issue(opening + (woven(t_h, products) if t_h else products))
             else:
                 issue(t_h)
+            if step == 0:
+                spread_b2()
+            if step == 1:
+                spread_b3()
             if due(step):
                 copy_ht(step)
             if due(step - 1):

@@ -101,12 +101,17 @@ def tile_switchnet_fstar_pb_t_e_kernel(tc, h_switch, k2, b2, k3_words, k3_scales
                 in_=y_ps[:].rearrange("b (p u e) -> b u p e", u=PAIRS, e=2),
             )
 
-        def spread_b3():
-            for half in range(HALVES):
-                cols = slice(half * BANK, (half + 1) * BANK)
-                y_ps = psum_y.tile([P, BANK], F32)
-                nc.tensor.matmul(y_ps[:], lhsT=ones[:], rhs=b3_row0[:, cols], start=True, stop=True)
-                nc.vector.tensor_copy(out=b3_f32[:, cols], in_=y_ps[:])
+        b3_ps_of = {}
+
+        def spread_b3(half):
+            cols = slice(half * BANK, (half + 1) * BANK)
+            y_ps = psum_y.tile([P, BANK], F32)
+            nc.tensor.matmul(y_ps[:], lhsT=ones[:], rhs=b3_row0[:, cols], start=True, stop=True)
+            b3_ps_of[half] = y_ps
+
+        def take_b3(half):
+            cols = slice(half * BANK, (half + 1) * BANK)
+            nc.vector.tensor_copy(out=b3_f32[:, cols], in_=b3_ps_of[half][:])
 
         ht_of = {}
         ht_ps_of = {}
@@ -252,8 +257,8 @@ def tile_switchnet_fstar_pb_t_e_kernel(tc, h_switch, k2, b2, k3_words, k3_scales
                 issue(t_h)
             if step == 0:
                 spread_b2()
-            if step == 1:
-                spread_b3()
+                for half in range(HALVES):
+                    spread_b3(half)
             if due(step):
                 copy_ht(step)
             if due(step - 1):
@@ -272,3 +277,5 @@ def tile_switchnet_fstar_pb_t_e_kernel(tc, h_switch, k2, b2, k3_words, k3_scales
                 copy_gt(step - 2)
             if due(step - 1):
                 take_g(step - 1, 1)
+            if 1 <= step <= HALVES:
+                take_b3(step - 1)

@@ -138,7 +138,10 @@ def tile_switchnet_fstar_pb_t_e_kernel(tc, h_switch, k2, b2, k3_words, k3_scales
 
         def copy_ht(r):
             ht = ht_pool.tile([P, ROUND_TILES, GROUPS, P], BF16)
-            nc.scalar.copy(out=ht[:], in_=ht_ps_of[r][:])
+            nc.scalar.copy(
+                out=ht[:].rearrange("i c j b -> i (c j b)").bitcast(F32),
+                in_=ht_ps_of[r][:].rearrange("i c j b -> i (c j b)").bitcast(F32),
+            )
             ht_of[r] = ht
 
         def products_of(r, c):

@@ -27,6 +27,7 @@ ROUND_TILES = 2
 CHUNK_ROUNDS = CHUNK_TILES // ROUND_TILES
 ROUNDS = CHUNKS * CHUNK_ROUNDS
 TENSOR_BIAS_TILE = 1
+WARM_COLUMNS = 480
 SPREADS = 3
 
 FLOPS = 2 * BATCH * (GROUPS * R * R + K3 * L3)
@@ -56,6 +57,7 @@ def tile_switchnet_fstar_pb_t_e_kernel(tc, h_switch, k2, b2, k3_words, k3_scales
         k3_plane = keep.tile([P, L3], U8, align_bytes=64)
         b2_sorted = keep.tile([P, K3], F32)
         b3_f32 = keep.tile([P, L3], F32)
+        warm = keep.tile([P, WARM_COLUMNS], F32)
         ident_bf16 = keep.tile([P, P], BF16)
         ident_f32 = keep.tile([P, P], F32)
         ones = keep.tile([P, P], BF16)
@@ -66,12 +68,16 @@ def tile_switchnet_fstar_pb_t_e_kernel(tc, h_switch, k2, b2, k3_words, k3_scales
             cols = slice(first_tile, first_tile + tiles)
             nc.sync.dma_start(out=h_sb[:, n, cols, :], in_=h_chunks[n][:, cols, :])
 
+        nc.vector.memset(warm[:], 0.0)
         nc.vector.memset(k3_plane[:].bitcast(I32), 0)
         nc.vector.memset(b2_row0[:], 0.0)
         nc.vector.memset(b3_row0[:], 0.0)
         nc.vector.memset(ones[:], 1.0)
         make_identity(nc, ident_bf16[:])
         make_identity(nc, ident_f32[:])
+
+        warm_ps = psum_y.tile([P, BANK], F32, name="y_ps")
+        nc.tensor.matmul(warm_ps[:, :WARM_COLUMNS], lhsT=warm[:, :P], rhs=warm[:], start=True, stop=True)
 
         nc.scalar.dma_start(out=b2_row0[0:1, :], in_=b2.rearrange("o j r -> o (j r)"))
         nc.scalar.dma_start(out=b3_row0[0:1, :], in_=b3.rearrange("o j l -> o (j l)"))

@@ -27,7 +27,7 @@ ROUND_TILES = 2
 CHUNK_ROUNDS = CHUNK_TILES // ROUND_TILES
 ROUNDS = CHUNKS * CHUNK_ROUNDS
 TENSOR_BIAS_TILE = 1
-WARM_COLUMNS = 480
+WARM_UPS = 3
 SPREADS = 3
 
 FLOPS = 2 * BATCH * (GROUPS * R * R + K3 * L3)
@@ -53,11 +53,11 @@ def tile_switchnet_fstar_pb_t_e_kernel(tc, h_switch, k2, b2, k3_words, k3_scales
 
         h_sb = keep.tile([P, CHUNKS, CHUNK_TILES, K3], BF16)
         k2_sb = keep.tile([P, GROUPS, R], BF16)
-        k3_codes = keep.tile([P, L3], U32, align_bytes=64)
-        k3_plane = keep.tile([P, L3], U8, align_bytes=64)
+        k3_codes = keep.tile([P, L3], U32, align_bytes=256)
+        k3_plane = keep.tile([P, L3], U8, align_bytes=256)
         b2_sorted = keep.tile([P, K3], F32)
         b3_f32 = keep.tile([P, L3], F32)
-        warm = keep.tile([P, WARM_COLUMNS], F32)
+        warm = keep.tile([P, P], F32)
         ident_bf16 = keep.tile([P, P], BF16)
         ident_f32 = keep.tile([P, P], F32)
         ones = keep.tile([P, P], BF16)
@@ -77,7 +77,8 @@ def tile_switchnet_fstar_pb_t_e_kernel(tc, h_switch, k2, b2, k3_words, k3_scales
         make_identity(nc, ident_f32[:])
 
         warm_ps = psum_y.tile([P, BANK], F32, name="y_ps")
-        nc.tensor.matmul(warm_ps[:, :WARM_COLUMNS], lhsT=warm[:, :P], rhs=warm[:], start=True, stop=True)
+        for w in range(WARM_UPS):
+            nc.tensor.matmul(warm_ps[:, w * P : (w + 1) * P], lhsT=warm[:], rhs=warm[:], start=True, stop=True)
 
         nc.scalar.dma_start(out=b2_row0[0:1, :], in_=b2.rearrange("o j r -> o (j r)"))
         nc.scalar.dma_start(out=b3_row0[0:1, :], in_=b3.rearrange("o j l -> o (j l)"))
@@ -221,8 +222,8 @@ def tile_switchnet_fstar_pb_t_e_kernel(tc, h_switch, k2, b2, k3_words, k3_scales
 
         def quantise(r):
             grouped = grouped_of[r]
-            g_codes = mx_pool.tile([P, ROUND_TILES * P], U32, align_bytes=64)
-            g_plane = mx_pool.tile([P, ROUND_TILES * P], U8, align_bytes=64)
+            g_codes = mx_pool.tile([P, ROUND_TILES * P], U32, align_bytes=256)
+            g_plane = mx_pool.tile([P, ROUND_TILES * P], U8, align_bytes=256)
             nc.vector.quantize_mx(out=g_codes[:].bitcast(FP8X4), scales=g_plane[:], in_=grouped[:])
             codes_of[r] = g_codes
             plane_of[r] = g_plane

@@ -27,7 +27,8 @@ ROUND_TILES = 2
 CHUNK_ROUNDS = CHUNK_TILES // ROUND_TILES
 ROUNDS = CHUNKS * CHUNK_ROUNDS
 TENSOR_BIAS_TILE = 1
-WARM_UPS = 3
+WARM_UPS, WARM_COLUMNS = 3, 160
+RAMP = 2
 SPREADS = 3
 
 FLOPS = 2 * BATCH * (GROUPS * R * R + K3 * L3)
@@ -57,7 +58,7 @@ def tile_switchnet_fstar_pb_t_e_kernel(tc, h_switch, k2, b2, k3_words, k3_scales
         k3_plane = keep.tile([P, L3], U8, align_bytes=256)
         b2_sorted = keep.tile([P, K3], F32)
         b3_f32 = keep.tile([P, L3], F32)
-        warm = keep.tile([P, P], F32)
+        warm = keep.tile([P, WARM_COLUMNS], F32)
         ident_bf16 = keep.tile([P, P], BF16)
         ident_f32 = keep.tile([P, P], F32)
         ones = keep.tile([P, P], BF16)
@@ -78,12 +79,14 @@ def tile_switchnet_fstar_pb_t_e_kernel(tc, h_switch, k2, b2, k3_words, k3_scales
 
         warm_ps = psum_y.tile([P, BANK], F32, name="y_ps")
         for w in range(WARM_UPS):
-            nc.tensor.matmul(warm_ps[:, w * P : (w + 1) * P], lhsT=warm[:], rhs=warm[:], start=True, stop=True)
+            cols = slice(w * WARM_COLUMNS, (w + 1) * WARM_COLUMNS)
+            nc.tensor.matmul(warm_ps[:, cols], lhsT=warm[:, :P], rhs=warm[:], start=True, stop=True)
 
         nc.scalar.dma_start(out=b2_row0[0:1, :], in_=b2.rearrange("o j r -> o (j r)"))
         nc.scalar.dma_start(out=b3_row0[0:1, :], in_=b3.rearrange("o j l -> o (j l)"))
 
-        load_h(0, 0, ROUND_TILES)
+        for c in range(ROUND_TILES):
+            load_h(0, c, 1)
         nc.sync.dma_start(out=k2_sb[:], in_=k2.rearrange("j i r -> i j r"))
         load_h(0, ROUND_TILES, ROUND_TILES)
         for quadrant in range(4):
@@ -132,11 +135,15 @@ def tile_switchnet_fstar_pb_t_e_kernel(tc, h_switch, k2, b2, k3_words, k3_scales
         def transposes_of_h(r):
             n, q = divmod(r, CHUNK_ROUNDS)
             ht_ps = psum_ht.tile([P, ROUND_TILES, GROUPS, P], BF16)
-            ht_ps_of[r] = ht_ps
+            banks = [ht_ps, ht_ps]
+            if r < RAMP:
+                y_ps = psum_y.tile([P, ROUND_TILES, GROUPS, P], BF16)
+                banks = [ht_ps, y_ps]
+            ht_ps_of[r] = banks
 
             def one(c, j):
                 nc.tensor.transpose(
-                    ht_ps[:, c, j, :],
+                    banks[c][:, c, j, :],
                     h_sb[:, n, q * ROUND_TILES + c, j * R : (j + 1) * R],
                     ident_bf16[:],
                 )
@@ -145,11 +152,20 @@ def tile_switchnet_fstar_pb_t_e_kernel(tc, h_switch, k2, b2, k3_words, k3_scales
 
         def copy_ht(r):
             ht = ht_pool.tile([P, ROUND_TILES, GROUPS, P], BF16)
-            nc.scalar.copy(
-                out=ht[:].rearrange("i c j b -> i (c j b)").bitcast(F32),
-                in_=ht_ps_of[r][:].rearrange("i c j b -> i (c j b)").bitcast(F32),
-            )
             ht_of[r] = ht
+            banks = ht_ps_of[r]
+            if r < RAMP:
+                for c in range(ROUND_TILES):
+                    copy = nc.vector.tensor_copy if (r, c) == (0, 1) else nc.scalar.copy
+                    copy(
+                        out=ht[:, c, :, :].rearrange("i j b -> i (j b)").bitcast(F32),
+                        in_=banks[c][:, c, :, :].rearrange("i j b -> i (j b)").bitcast(F32),
+                    )
+            else:
+                nc.scalar.copy(
+                    out=ht[:].rearrange("i c j b -> i (c j b)").bitcast(F32),
+                    in_=banks[0][:].rearrange("i c j b -> i (c j b)").bitcast(F32),
+                )
 
         def products_of(r, c):
             ht = ht_of[r]
@@ -260,11 +276,16 @@ def tile_switchnet_fstar_pb_t_e_kernel(tc, h_switch, k2, b2, k3_words, k3_scales
 
         for step in range(ROUNDS + 4):
             t_h = transposes_of_h(step) if due(step) else []
-            if due(step - 1):
-                opening, products = products_of(step - 1, 0)
-                issue(opening + (woven(t_h, products) if t_h else products))
+            t_g = transposes_of_g(step - 2) if due(step - 2) else []
+            firsts = [products_of(step - 1, c) if due(step - 1) else ([], []) for c in range(ROUND_TILES)]
+            if step < RAMP:
+                for c in range(ROUND_TILES):
+                    issue(t_h[c * GROUPS : (c + 1) * GROUPS])
+                    opening, products = firsts[c]
+                    issue(opening + products)
             else:
-                issue(t_h)
+                opening, products = firsts[0]
+                issue(opening + (woven(t_h, products) if t_h and products else t_h + products))
             if step == 0:
                 spread_b2()
                 for half in range(HALVES):
@@ -277,15 +298,12 @@ def tile_switchnet_fstar_pb_t_e_kernel(tc, h_switch, k2, b2, k3_words, k3_scales
                 quantise(step - 3)
             if due(step - 4):
                 second_matmul(step - 4)
-            t_g = transposes_of_g(step - 2) if due(step - 2) else []
-            if due(step - 1):
-                opening, products = products_of(step - 1, 1)
-                issue(opening + (woven(t_g, products) if t_g else products))
-            else:
-                issue(t_g)
-            if due(step - 2):
-                copy_gt(step - 2)
+            if step >= RAMP:
+                opening, products = firsts[1]
+                issue(opening + (woven(t_g, products) if t_g and products else t_g + products))
             if due(step - 1):
                 take_g(step - 1, 1)
+            if due(step - 2):
+                copy_gt(step - 2)
             if 1 <= step <= HALVES:
                 take_b3(step - 1)

@@ -28,7 +28,8 @@ CHUNK_ROUNDS = CHUNK_TILES // ROUND_TILES
 ROUNDS = CHUNKS * CHUNK_ROUNDS
 TENSOR_BIAS_TILE = 1
 WARM_UPS, WARM_COLUMNS = 3, 160
-RAMP = 2
+RAMP = 3
+FILL = 4
 SPREADS = 3
 
 FLOPS = 2 * BATCH * (GROUPS * R * R + K3 * L3)
@@ -70,10 +71,10 @@ def tile_switchnet_fstar_pb_t_e_kernel(tc, h_switch, k2, b2, k3_words, k3_scales
             nc.sync.dma_start(out=h_sb[:, n, cols, :], in_=h_chunks[n][:, cols, :])
 
         nc.vector.memset(warm[:], 0.0)
-        nc.vector.memset(k3_plane[:].bitcast(I32), 0)
-        nc.vector.memset(b2_row0[:], 0.0)
-        nc.vector.memset(b3_row0[:], 0.0)
+        nc.vector.memset(b2_row0[:].bitcast(F32), 0.0)
+        nc.vector.memset(b3_row0[:].bitcast(F32), 0.0)
         nc.vector.memset(ones[:], 1.0)
+        nc.vector.memset(k3_plane[:].bitcast(I32), 0)
         make_identity(nc, ident_bf16[:])
         make_identity(nc, ident_f32[:])
 
@@ -82,13 +83,16 @@ def tile_switchnet_fstar_pb_t_e_kernel(tc, h_switch, k2, b2, k3_words, k3_scales
             cols = slice(w * WARM_COLUMNS, (w + 1) * WARM_COLUMNS)
             nc.tensor.matmul(warm_ps[:, cols], lhsT=warm[:, :P], rhs=warm[:], start=True, stop=True)
 
-        nc.scalar.dma_start(out=b2_row0[0:1, :], in_=b2.rearrange("o j r -> o (j r)"))
-        nc.scalar.dma_start(out=b3_row0[0:1, :], in_=b3.rearrange("o j l -> o (j l)"))
+        table = keep.tile([P, 1], F32)
+        nc.scalar.copy(out=table[:], in_=warm[:, 0:1])
 
         for c in range(ROUND_TILES):
             load_h(0, c, 1)
         nc.sync.dma_start(out=k2_sb[:], in_=k2.rearrange("j i r -> i j r"))
-        load_h(0, ROUND_TILES, ROUND_TILES)
+        nc.sync.dma_start(out=b2_row0[0:1, :], in_=b2.rearrange("o j r -> o (j r)"))
+        nc.sync.dma_start(out=b3_row0[0:1, :], in_=b3.rearrange("o j l -> o (j l)"))
+        for r in range(1, CHUNK_ROUNDS):
+            load_h(0, r * ROUND_TILES, ROUND_TILES)
         for quadrant in range(4):
             nc.sync.dma_start(
                 out=k3_plane[32 * quadrant : 32 * quadrant + 4, :].bitcast(I32),
@@ -98,30 +102,31 @@ def tile_switchnet_fstar_pb_t_e_kernel(tc, h_switch, k2, b2, k3_words, k3_scales
             out=k3_codes[:].bitcast(I32),
             in_=k3_words[0].rearrange("p n t -> p (n t)").bitcast(I32),
         )
-        for r in range(2, CHUNK_ROUNDS):
-            load_h(0, r * ROUND_TILES, ROUND_TILES)
         for n in range(1, CHUNKS):
             load_h(n, 0, CHUNK_TILES)
+
+        bias_ps_of = {}
 
         def spread_b2():
             y_ps = psum_y.tile([P, BANK], F32)
             nc.tensor.matmul(y_ps[:], lhsT=ones[:], rhs=b2_row0[:], start=True, stop=True)
+            bias_ps_of["b2"] = y_ps
+
+        def take_b2():
             nc.vector.tensor_copy(
                 out=b2_sorted[:].rearrange("b (u p e) -> b u p e", u=PAIRS, e=2),
-                in_=y_ps[:].rearrange("b (p u e) -> b u p e", u=PAIRS, e=2),
+                in_=bias_ps_of["b2"][:].rearrange("b (p u e) -> b u p e", u=PAIRS, e=2),
             )
-
-        b3_ps_of = {}
 
         def spread_b3(half):
             cols = slice(half * BANK, (half + 1) * BANK)
             y_ps = psum_y.tile([P, BANK], F32)
             nc.tensor.matmul(y_ps[:], lhsT=ones[:], rhs=b3_row0[:, cols], start=True, stop=True)
-            b3_ps_of[half] = y_ps
+            bias_ps_of[half] = y_ps
 
         def take_b3(half):
             cols = slice(half * BANK, (half + 1) * BANK)
-            nc.vector.tensor_copy(out=b3_f32[:, cols], in_=b3_ps_of[half][:])
+            (nc.scalar.copy if half == 0 else nc.vector.tensor_copy)(out=b3_f32[:, cols], in_=bias_ps_of[half][:])
 
         ht_of = {}
         ht_ps_of = {}
@@ -283,15 +288,18 @@ def tile_switchnet_fstar_pb_t_e_kernel(tc, h_switch, k2, b2, k3_words, k3_scales
                     issue(t_h[c * GROUPS : (c + 1) * GROUPS])
                     opening, products = firsts[c]
                     issue(opening + products)
+                issue(t_g)
             else:
                 opening, products = firsts[0]
-                issue(opening + (woven(t_h, products) if t_h and products else t_h + products))
+                issue(opening + (woven(t_h, products) if t_h and products and step >= FILL else t_h + products))
             if step == 0:
                 spread_b2()
                 for half in range(HALVES):
                     spread_b3(half)
             if due(step):
                 copy_ht(step)
+            if step == 0:
+                take_b2()
             if due(step - 1):
                 take_g(step - 1, 0)
             if due(step - 3):

@@ -27,9 +27,7 @@ ROUND_TILES = 2
 CHUNK_ROUNDS = CHUNK_TILES // ROUND_TILES
 ROUNDS = CHUNKS * CHUNK_ROUNDS
 TENSOR_BIAS_TILE = 1
-WARM_UPS, WARM_COLUMNS = 3, 160
-RAMP = 3
-FILL = 4
+WARM_UPS, WARM_COLUMNS = 3, 128
 SPREADS = 3
 
 FLOPS = 2 * BATCH * (GROUPS * R * R + K3 * L3)
@@ -47,9 +45,8 @@ def tile_switchnet_fstar_pb_t_e_kernel(tc, h_switch, k2, b2, k3_words, k3_scales
         grouped_pool = ctx.enter_context(tc.tile_pool(name="grouped", bufs=2))
         mx_pool = ctx.enter_context(tc.tile_pool(name="mx", bufs=3))
         y_pool = ctx.enter_context(tc.tile_pool(name="y", bufs=4))
-        psum_ht = ctx.enter_context(tc.psum_pool(name="psum_ht", bufs=1))
         psum_g = ctx.enter_context(tc.psum_pool(name="psum_g", bufs=ROUND_TILES))
-        psum_gt = ctx.enter_context(tc.psum_pool(name="psum_gt", bufs=1))
+        psum_t = ctx.enter_context(tc.psum_pool(name="psum_t", bufs=1))
         psum_y = ctx.enter_context(tc.psum_pool(name="psum_y", bufs=ROUND_TILES * HALVES))
         ctx.enter_context(tc.manual_schedule())
 
@@ -129,48 +126,38 @@ def tile_switchnet_fstar_pb_t_e_kernel(tc, h_switch, k2, b2, k3_words, k3_scales
             (nc.scalar.copy if half == 0 else nc.vector.tensor_copy)(out=b3_f32[:, cols], in_=bias_ps_of[half][:])
 
         ht_of = {}
-        ht_ps_of = {}
         g_ps_of = {}
-        gt_ps_of = {}
         g_of = {}
         grouped_of = {}
         codes_of = {}
         plane_of = {}
 
-        def transposes_of_h(r):
-            n, q = divmod(r, CHUNK_ROUNDS)
-            ht_ps = psum_ht.tile([P, ROUND_TILES, GROUPS, P], BF16)
-            banks = [ht_ps, ht_ps]
-            if r < RAMP:
-                y_ps = psum_y.tile([P, ROUND_TILES, GROUPS, P], BF16)
-                banks = [ht_ps, y_ps]
-            ht_ps_of[r] = banks
+        def bank_for(step, c):
+            bank = psum_t.tile([P, BANK], F32, name="half%d" % c)
+            return bank
 
-            def one(c, j):
+        def transposes_of_h(r, c, bank):
+            n, q = divmod(r, CHUNK_ROUNDS)
+            ht_ps = bank[:, : BANK // 2].bitcast(BF16).rearrange("i (j b) -> i j b", j=GROUPS)
+
+            def one(j):
                 nc.tensor.transpose(
-                    banks[c][:, c, j, :],
+                    ht_ps[:, j, :],
                     h_sb[:, n, q * ROUND_TILES + c, j * R : (j + 1) * R],
                     ident_bf16[:],
                 )
 
-            return [(one, c, j) for c in range(ROUND_TILES) for j in range(GROUPS)]
+            return [(one, j) for j in range(GROUPS)]
 
-        def copy_ht(r):
-            ht = ht_pool.tile([P, ROUND_TILES, GROUPS, P], BF16)
-            ht_of[r] = ht
-            banks = ht_ps_of[r]
-            if r < RAMP:
-                for c in range(ROUND_TILES):
-                    copy = nc.vector.tensor_copy if (r, c) == (0, 1) else nc.scalar.copy
-                    copy(
-                        out=ht[:, c, :, :].rearrange("i j b -> i (j b)").bitcast(F32),
-                        in_=banks[c][:, c, :, :].rearrange("i j b -> i (j b)").bitcast(F32),
-                    )
-            else:
-                nc.scalar.copy(
-                    out=ht[:].rearrange("i c j b -> i (c j b)").bitcast(F32),
-                    in_=banks[0][:].rearrange("i c j b -> i (c j b)").bitcast(F32),
-                )
+        def copy_ht(r, c, bank):
+            if c == 0:
+                ht = ht_pool.tile([P, ROUND_TILES, GROUPS, P], BF16)
+                ht_of[r] = ht
+            copy = nc.vector.tensor_copy if (r, c) == (0, 1) else nc.scalar.copy
+            copy(
+                out=ht_of[r][:, c, :, :].rearrange("i j b -> i (j b)").bitcast(F32),
+                in_=bank[:, : BANK // 2],
+            )
 
         def products_of(r, c):
             ht = ht_of[r]
@@ -210,34 +197,35 @@ def tile_switchnet_fstar_pb_t_e_kernel(tc, h_switch, k2, b2, k3_words, k3_scales
                     op=ADD,
                 )
 
-        def transposes_of_g(r):
-            g = g_of[r]
-            gt_ps = psum_gt.tile([P, ROUND_TILES, PAIRS, P], F32)
-            gt_ps_of[r] = gt_ps
+        def transposes_of_g(r, c, bank):
+            g_words = g_of[r][:, c, :].bitcast(F32)
+            gt_ps = bank[:, BANK // 2 :].rearrange("p (u b) -> p u b", u=PAIRS)
 
-            def one(c, u):
-                g_words = g[:, c, :].bitcast(F32)
-                nc.tensor.transpose(gt_ps[:, c, u, :], g_words[:, u * P : (u + 1) * P], ident_f32[:])
+            def one(u):
+                nc.tensor.transpose(gt_ps[:, u, :], g_words[:, u * P : (u + 1) * P], ident_f32[:])
 
-            return [(one, c, u) for c in range(ROUND_TILES) for u in range(PAIRS)]
+            return [(one, u) for u in range(PAIRS)]
 
-        def copy_gt(r):
-            grouped = grouped_pool.tile([P, ROUND_TILES * P * 4], BF16, align_bytes=64)
+        def copy_gt(r, c, bank):
+            if c == 0:
+                grouped = grouped_pool.tile([P, ROUND_TILES * P * 4], BF16, align_bytes=64)
+                grouped_of[r] = grouped
             nc.scalar.copy(
-                out=grouped[:].bitcast(F32).rearrange("p (c b u) -> p c b u", c=ROUND_TILES, u=PAIRS),
-                in_=gt_ps_of[r][:].rearrange("p c u b -> p c b u"),
+                out=grouped_of[r][:].bitcast(F32).rearrange("p (c b u) -> p c b u", c=ROUND_TILES, u=PAIRS)[:, c, :, :],
+                in_=bank[:, BANK // 2 :].rearrange("p (u b) -> p b u", u=PAIRS),
             )
-            grouped_of[r] = grouped
 
         def issue(calls):
             for call in calls:
                 call[0](*call[1:])
 
         def woven(transposes, matmuls):
-            share = len(transposes) // len(matmuls)
+            if not matmuls:
+                return transposes
             out_list = []
             for k in range(len(matmuls)):
-                out_list.extend(transposes[k * share : (k + 1) * share])
+                first, last = k * len(transposes) // len(matmuls), (k + 1) * len(transposes) // len(matmuls)
+                out_list.extend(transposes[first:last])
                 out_list.append(matmuls[k])
             return out_list
 
@@ -280,38 +268,34 @@ def tile_switchnet_fstar_pb_t_e_kernel(tc, h_switch, k2, b2, k3_words, k3_scales
             return 0 <= r < ROUNDS
 
         for step in range(ROUNDS + 4):
-            t_h = transposes_of_h(step) if due(step) else []
-            t_g = transposes_of_g(step - 2) if due(step - 2) else []
-            firsts = [products_of(step - 1, c) if due(step - 1) else ([], []) for c in range(ROUND_TILES)]
-            if step < RAMP:
-                for c in range(ROUND_TILES):
-                    issue(t_h[c * GROUPS : (c + 1) * GROUPS])
-                    opening, products = firsts[c]
-                    issue(opening + products)
-                issue(t_g)
-            else:
-                opening, products = firsts[0]
-                issue(opening + (woven(t_h, products) if t_h and products and step >= FILL else t_h + products))
-            if step == 0:
-                spread_b2()
-                for half in range(HALVES):
-                    spread_b3(half)
-            if due(step):
-                copy_ht(step)
-            if step == 0:
-                take_b2()
-            if due(step - 1):
-                take_g(step - 1, 0)
-            if due(step - 3):
-                quantise(step - 3)
-            if due(step - 4):
-                second_matmul(step - 4)
-            if step >= RAMP:
-                opening, products = firsts[1]
-                issue(opening + (woven(t_g, products) if t_g and products else t_g + products))
-            if due(step - 1):
-                take_g(step - 1, 1)
-            if due(step - 2):
-                copy_gt(step - 2)
+            for c in range(ROUND_TILES):
+                bank = bank_for(step, c) if due(step) or due(step - 2) else None
+                transposes = transposes_of_h(step, c, bank) if due(step) else []
+                if due(step - 2):
+                    transposes = transposes + transposes_of_g(step - 2, c, bank)
+                opening, products = products_of(step - 1, c) if due(step - 1) else ([], [])
+                issue(opening + woven(transposes, products))
+                if due(step):
+                    copy_ht(step, c, bank)
+                if step == 0 and c == 0:
+                    spread_b2()
+                    take_b2()
+                if step == 0 and c == 1:
+                    for half in range(HALVES):
+                        spread_b3(half)
+                if due(step - 1) and c == 0:
+                    take_g(step - 1, 0)
+                if c == 0:
+                    if due(step - 2):
+                        copy_gt(step - 2, c, bank)
+                    if due(step - 3):
+                        quantise(step - 3)
+                    if due(step - 4):
+                        second_matmul(step - 4)
+                else:
+                    if due(step - 1):
+                        take_g(step - 1, 1)
+                    if due(step - 2):
+                        copy_gt(step - 2, c, bank)
             if 1 <= step <= HALVES:
                 take_b3(step - 1)

@@ -123,7 +123,7 @@ def tile_switchnet_fstar_pb_t_e_kernel(tc, h_switch, k2, b2, k3_words, k3_scales
 
         def take_b3(half):
             cols = slice(half * BANK, (half + 1) * BANK)
-            (nc.scalar.copy if half == 0 else nc.vector.tensor_copy)(out=b3_f32[:, cols], in_=bias_ps_of[half][:])
+            nc.scalar.copy(out=b3_f32[:, cols], in_=bias_ps_of[half][:])
 
         ht_of = {}
         g_ps_of = {}
@@ -270,19 +270,16 @@ def tile_switchnet_fstar_pb_t_e_kernel(tc, h_switch, k2, b2, k3_words, k3_scales
         for step in range(ROUNDS + 4):
             for c in range(ROUND_TILES):
                 bank = bank_for(step, c) if due(step) or due(step - 2) else None
-                transposes = transposes_of_h(step, c, bank) if due(step) else []
-                if due(step - 2):
-                    transposes = transposes + transposes_of_g(step - 2, c, bank)
+                transposes = transposes_of_g(step - 2, c, bank) if due(step - 2) else []
+                if due(step):
+                    transposes = transposes + transposes_of_h(step, c, bank)
                 opening, products = products_of(step - 1, c) if due(step - 1) else ([], [])
                 issue(opening + woven(transposes, products))
                 if due(step):
                     copy_ht(step, c, bank)
-                if step == 0 and c == 0:
+                if step == 0 and c == 1:
                     spread_b2()
                     take_b2()
-                if step == 0 and c == 1:
-                    for half in range(HALVES):
-                        spread_b3(half)
                 if due(step - 1) and c == 0:
                     take_g(step - 1, 0)
                 if c == 0:
@@ -297,5 +294,7 @@ def tile_switchnet_fstar_pb_t_e_kernel(tc, h_switch, k2, b2, k3_words, k3_scales
                         take_g(step - 1, 1)
                     if due(step - 2):
                         copy_gt(step - 2, c, bank)
-            if 1 <= step <= HALVES:
-                take_b3(step - 1)
+            if 2 <= step < 2 + HALVES:
+                take_b3(step - 2)
+            if 1 <= step < 1 + HALVES:
+                spread_b3(step - 1)

@@ -28,6 +28,7 @@ CHUNK_ROUNDS = CHUNK_TILES // ROUND_TILES
 ROUNDS = CHUNKS * CHUNK_ROUNDS
 TENSOR_BIAS_TILE = 1
 WARM_UPS, WARM_COLUMNS = 3, 128
+FILL = 4
 SPREADS = 3
 
 FLOPS = 2 * BATCH * (GROUPS * R * R + K3 * L3)
@@ -204,7 +205,11 @@ def tile_switchnet_fstar_pb_t_e_kernel(tc, h_switch, k2, b2, k3_words, k3_scales
             def one(u):
                 nc.tensor.transpose(gt_ps[:, u, :], g_words[:, u * P : (u + 1) * P], ident_f32[:])
 
-            return [(one, u) for u in range(PAIRS)]
+            def both():
+                for u in range(PAIRS):
+                    one(u)
+
+            return [(both,)]
 
         def copy_gt(r, c, bank):
             if c == 0:
@@ -270,9 +275,9 @@ def tile_switchnet_fstar_pb_t_e_kernel(tc, h_switch, k2, b2, k3_words, k3_scales
         for step in range(ROUNDS + 4):
             for c in range(ROUND_TILES):
                 bank = bank_for(step, c) if due(step) or due(step - 2) else None
-                transposes = transposes_of_g(step - 2, c, bank) if due(step - 2) else []
-                if due(step):
-                    transposes = transposes + transposes_of_h(step, c, bank)
+                of_h = transposes_of_h(step, c, bank) if due(step) else []
+                of_g = transposes_of_g(step - 2, c, bank) if due(step - 2) else []
+                transposes = of_h + of_g if step < FILL else of_g + of_h
                 opening, products = products_of(step - 1, c) if due(step - 1) else ([], [])
                 issue(opening + woven(transposes, products))
                 if due(step):

from contextlib import ExitStack

import concourse.mybir as mybir
from concourse.masks import make_identity

F32 = mybir.dt.float32
BF16 = mybir.dt.bfloat16
I32 = mybir.dt.int32
U32 = mybir.dt.uint32
U8 = mybir.dt.uint8
FP8X4 = mybir.dt.float8_e4m3fn_x4
ADD = mybir.AluOpType.add

P = 128
BATCH = 4096
GROUPS = 4
R = 128
K3 = GROUPS * R
L3 = 1024
BANK = 512
HALVES = L3 // BANK
PAIRS = 2

CHUNK_TILES = 8
CHUNKS = BATCH // (P * CHUNK_TILES)
ROUND_TILES = 2
CHUNK_ROUNDS = CHUNK_TILES // ROUND_TILES
ROUNDS = CHUNKS * CHUNK_ROUNDS
TENSOR_BIAS_TILE = 1
WARM_UPS, WARM_COLUMNS = 3, 128
FILL = 4
SPREADS = 3

FLOPS = 2 * BATCH * (GROUPS * R * R + K3 * L3)


def tile_switchnet_fstar_pb_t_e_kernel(tc, h_switch, k2, b2, k3_words, k3_scales, b3, out):
    nc = tc.nc
    h_chunks = h_switch.rearrange("(n p c) j i -> n p c (j i)", p=P, c=CHUNK_TILES)
    out_chunks = out.rearrange("(n p c) x y z -> n p c (x y z)", p=P, c=CHUNK_TILES)

    with ExitStack() as ctx:
        keep = ctx.enter_context(tc.tile_pool(name="keep", bufs=1))
        ht_pool = ctx.enter_context(tc.tile_pool(name="ht", bufs=3))
        g_pool = ctx.enter_context(tc.tile_pool(name="g", bufs=4))
        grouped_pool = ctx.enter_context(tc.tile_pool(name="grouped", bufs=2))
        mx_pool = ctx.enter_context(tc.tile_pool(name="mx", bufs=3))
        y_pool = ctx.enter_context(tc.tile_pool(name="y", bufs=4))
        psum_g = ctx.enter_context(tc.psum_pool(name="psum_g", bufs=ROUND_TILES))
        psum_t = ctx.enter_context(tc.psum_pool(name="psum_t", bufs=1))
        psum_y = ctx.enter_context(tc.psum_pool(name="psum_y", bufs=ROUND_TILES * HALVES))
        ctx.enter_context(tc.manual_schedule())

        h_sb = keep.tile([P, CHUNKS, CHUNK_TILES, K3], BF16)
        k2_sb = keep.tile([P, GROUPS, R], BF16)
        k3_codes = keep.tile([P, L3], U32, align_bytes=256)
        k3_plane = keep.tile([P, L3], U8, align_bytes=256)
        b2_sorted = keep.tile([P, K3], F32)
        b3_f32 = keep.tile([P, L3], F32)
        warm = keep.tile([P, WARM_COLUMNS], F32)
        ident_bf16 = keep.tile([P, P], BF16)
        ident_f32 = keep.tile([P, P], F32)
        ones = keep.tile([P, P], BF16)
        b2_row0 = keep.tile([P, K3], BF16)
        b3_row0 = keep.tile([P, L3], BF16)

        def load_h(n, first_tile, tiles):
            cols = slice(first_tile, first_tile + tiles)
            nc.sync.dma_start(out=h_sb[:, n, cols, :], in_=h_chunks[n][:, cols, :])

        nc.vector.memset(warm[:], 0.0)
        nc.vector.memset(b2_row0[:].bitcast(F32), 0.0)
        nc.vector.memset(b3_row0[:].bitcast(F32), 0.0)
        nc.vector.memset(ones[:], 1.0)
        nc.vector.memset(k3_plane[:].bitcast(I32), 0)
        make_identity(nc, ident_bf16[:])
        make_identity(nc, ident_f32[:])

        warm_ps = psum_y.tile([P, BANK], F32, name="y_ps")
        for w in range(WARM_UPS):
            cols = slice(w * WARM_COLUMNS, (w + 1) * WARM_COLUMNS)
            nc.tensor.matmul(warm_ps[:, cols], lhsT=warm[:, :P], rhs=warm[:], start=True, stop=True)

        table = keep.tile([P, 1], F32)
        nc.scalar.copy(out=table[:], in_=warm[:, 0:1])

        for c in range(ROUND_TILES):
            load_h(0, c, 1)
        nc.sync.dma_start(out=k2_sb[:], in_=k2.rearrange("j i r -> i j r"))
        nc.sync.dma_start(out=b2_row0[0:1, :], in_=b2.rearrange("o j r -> o (j r)"))
        nc.sync.dma_start(out=b3_row0[0:1, :], in_=b3.rearrange("o j l -> o (j l)"))
        for r in range(1, CHUNK_ROUNDS):
            load_h(0, r * ROUND_TILES, ROUND_TILES)
        for quadrant in range(4):
            nc.sync.dma_start(
                out=k3_plane[32 * quadrant : 32 * quadrant + 4, :].bitcast(I32),
                in_=k3_scales[0, 4 * quadrant : 4 * quadrant + 4, :].bitcast(I32),
            )
        nc.sync.dma_start(
            out=k3_codes[:].bitcast(I32),
            in_=k3_words[0].rearrange("p n t -> p (n t)").bitcast(I32),
        )
        for n in range(1, CHUNKS):
            load_h(n, 0, CHUNK_TILES)

        bias_ps_of = {}

        def spread_b2():
            y_ps = psum_y.tile([P, BANK], F32)
            nc.tensor.matmul(y_ps[:], lhsT=ones[:], rhs=b2_row0[:], start=True, stop=True)
            bias_ps_of["b2"] = y_ps

        def take_b2():
            nc.vector.tensor_copy(
                out=b2_sorted[:].rearrange("b (u p e) -> b u p e", u=PAIRS, e=2),
                in_=bias_ps_of["b2"][:].rearrange("b (p u e) -> b u p e", u=PAIRS, e=2),
            )

        def spread_b3(half):
            cols = slice(half * BANK, (half + 1) * BANK)
            y_ps = psum_y.tile([P, BANK], F32)
            nc.tensor.matmul(y_ps[:], lhsT=ones[:], rhs=b3_row0[:, cols], start=True, stop=True)
            bias_ps_of[half] = y_ps

        def take_b3(half):
            cols = slice(half * BANK, (half + 1) * BANK)
            nc.scalar.copy(out=b3_f32[:, cols], in_=bias_ps_of[half][:])

        ht_of = {}
        g_ps_of = {}
        g_of = {}
        grouped_of = {}
        codes_of = {}
        plane_of = {}

        def bank_for(step, c):
            bank = psum_t.tile([P, BANK], F32, name="half%d" % c)
            return bank

        def transposes_of_h(r, c, bank):
            n, q = divmod(r, CHUNK_ROUNDS)
            ht_ps = bank[:, : BANK // 2].bitcast(BF16).rearrange("i (j b) -> i j b", j=GROUPS)

            def one(j):
                nc.tensor.transpose(
                    ht_ps[:, j, :],
                    h_sb[:, n, q * ROUND_TILES + c, j * R : (j + 1) * R],
                    ident_bf16[:],
                )

            return [(one, j) for j in range(GROUPS)]

        def copy_ht(r, c, bank):
            if c == 0:
                ht = ht_pool.tile([P, ROUND_TILES, GROUPS, P], BF16)
                ht_of[r] = ht
            copy = nc.vector.tensor_copy if (r, c) == (0, 1) else nc.scalar.copy
            copy(
                out=ht_of[r][:, c, :, :].rearrange("i j b -> i (j b)").bitcast(F32),
                in_=bank[:, : BANK // 2],
            )

        def products_of(r, c):
            ht = ht_of[r]
            g_ps = psum_g.tile([P, K3], F32)
            g_ps_of[r, c] = g_ps
            tensor_adds_b2 = c == TENSOR_BIAS_TILE and r >= SPREADS

            def bias():
                nc.tensor.matmul(g_ps[:], lhsT=ones[:], rhs=b2_row0[:], start=True, stop=False)

            def one(j):
                nc.tensor.matmul(
                    g_ps[:, j * R : (j + 1) * R],
                    lhsT=ht[:, c, j, :],
                    rhs=k2_sb[:, j, :],
                    start=not tensor_adds_b2,
                    stop=not tensor_adds_b2 or j == GROUPS - 1,
                )

            return ([(bias,)] if tensor_adds_b2 else []), [(one, j) for j in range(GROUPS)]

        def take_g(r, c):
            if r not in g_of:
                g_new = g_pool.tile([P, ROUND_TILES, K3], BF16)
                g_of[r] = g_new
            g = g_of[r]
            g_ps = g_ps_of[r, c]
            g_sorted = g[:, c, :].rearrange("b (u p e) -> b u p e", u=PAIRS, e=2)
            g_ps_sorted = g_ps[:].rearrange("b (p u e) -> b u p e", u=PAIRS, e=2)
            if c == TENSOR_BIAS_TILE and r >= SPREADS:
                nc.scalar.copy(out=g_sorted, in_=g_ps_sorted)
            else:
                nc.vector.tensor_tensor(
                    out=g_sorted,
                    in0=g_ps_sorted,
                    in1=b2_sorted[:].rearrange("b (u p e) -> b u p e", u=PAIRS, e=2),
                    op=ADD,
                )

        def transposes_of_g(r, c, bank):
            g_words = g_of[r][:, c, :].bitcast(F32)
            gt_ps = bank[:, BANK // 2 :].rearrange("p (u b) -> p u b", u=PAIRS)

            def one(u):
                nc.tensor.transpose(gt_ps[:, u, :], g_words[:, u * P : (u + 1) * P], ident_f32[:])

            def both():
                for u in range(PAIRS):
                    one(u)

            return [(both,)]

        def copy_gt(r, c, bank):
            if c == 0:
                grouped = grouped_pool.tile([P, ROUND_TILES * P * 4], BF16, align_bytes=64)
                grouped_of[r] = grouped
            nc.scalar.copy(
                out=grouped_of[r][:].bitcast(F32).rearrange("p (c b u) -> p c b u", c=ROUND_TILES, u=PAIRS)[:, c, :, :],
                in_=bank[:, BANK // 2 :].rearrange("p (u b) -> p b u", u=PAIRS),
            )

        def issue(calls):
            for call in calls:
                call[0](*call[1:])

        def woven(transposes, matmuls):
            if not matmuls:
                return transposes
            out_list = []
            for k in range(len(matmuls)):
                first, last = k * len(transposes) // len(matmuls), (k + 1) * len(transposes) // len(matmuls)
                out_list.extend(transposes[first:last])
                out_list.append(matmuls[k])
            return out_list

        def quantise(r):
            grouped = grouped_of[r]
            g_codes = mx_pool.tile([P, ROUND_TILES * P], U32, align_bytes=256)
            g_plane = mx_pool.tile([P, ROUND_TILES * P], U8, align_bytes=256)
            nc.vector.quantize_mx(out=g_codes[:].bitcast(FP8X4), scales=g_plane[:], in_=grouped[:])
            codes_of[r] = g_codes
            plane_of[r] = g_plane

        def second_matmul(r):
            n, q = divmod(r, CHUNK_ROUNDS)
            g_codes = codes_of[r]
            g_plane = plane_of[r]
            y = y_pool.tile([P, ROUND_TILES, L3], F32)
            for c in range(ROUND_TILES):
                samples = slice(c * P, (c + 1) * P)
                for half in range(HALVES):
                    cols = slice(half * BANK, (half + 1) * BANK)
                    y_ps = psum_y.tile([P, BANK], F32)
                    nc.tensor.matmul_mx(
                        out=y_ps[:],
                        lhsT=g_codes[:, samples].bitcast(FP8X4),
                        lhsT_scale=g_plane[:, samples],
                        rhs=k3_codes[:, cols].bitcast(FP8X4),
                        rhs_scale=k3_plane[:, cols],
                        start=True,
                        stop=True,
                    )
                    if c == 0 and half == 0:
                        nc.scalar.copy(out=y[:, c, cols], in_=y_ps[:])
                        nc.gpsimd.tensor_tensor(out=y[:, c, cols], in0=y[:, c, cols], in1=b3_f32[:, cols], op=ADD)
                    else:
                        nc.vector.tensor_tensor(out=y[:, c, cols], in0=y_ps[:], in1=b3_f32[:, cols], op=ADD)
            tiles = slice(q * ROUND_TILES, (q + 1) * ROUND_TILES)
            nc.sync.dma_start(out=out_chunks[n][:, tiles, :], in_=y[:])

        def due(r):
            return 0 <= r < ROUNDS

        for step in range(ROUNDS + 4):
            for c in range(ROUND_TILES):
                bank = bank_for(step, c) if due(step) or due(step - 2) else None
                of_h = transposes_of_h(step, c, bank) if due(step) else []
                of_g = transposes_of_g(step - 2, c, bank) if due(step - 2) else []
                transposes = of_h + of_g if step < FILL else of_g + of_h
                opening, products = products_of(step - 1, c) if due(step - 1) else ([], [])
                issue(opening + woven(transposes, products))
                if due(step):
                    copy_ht(step, c, bank)
                if step == 0 and c == 1:
                    spread_b2()
                    take_b2()
                if due(step - 1) and c == 0:
                    take_g(step - 1, 0)
                if c == 0:
                    if due(step - 2):
                        copy_gt(step - 2, c, bank)
                    if due(step - 3):
                        quantise(step - 3)
                    if due(step - 4):
                        second_matmul(step - 4)
                else:
                    if due(step - 1):
                        take_g(step - 1, 1)
                    if due(step - 2):
                        copy_gt(step - 2, c, bank)
            if 2 <= step < 2 + HALVES:
                take_b3(step - 2)
            if 1 <= step < 1 + HALVES:
                spread_b3(step - 1)
